import numpy as np
import ml_dtypes


def mxq(x, axis, fmt="e4m3"):
    dtype, down = {"e4m3": (ml_dtypes.float8_e4m3fn, 7), "e5m2": (ml_dtypes.float8_e5m2, 14)}[fmt]
    v = np.moveaxis(np.asarray(x, np.float32).astype(ml_dtypes.bfloat16).astype(np.float64), axis, -1)
    blocks = v.reshape(v.shape[:-1] + (-1, 32))
    amax = np.abs(blocks).max(-1, keepdims=True)
    byte = np.maximum(np.where(amax > 0, np.frexp(amax)[1] - 1 + 127, 0) - down, 1)
    scale = np.exp2(byte - 127.0)
    codes = (blocks / scale).astype(np.float32).astype(dtype).astype(np.float64)
    return np.moveaxis((codes * scale).reshape(v.shape), -1, axis)


WIDE = False


def mx_kscale(k):
    if not WIDE:
        return np.ones(k)
    levels = np.array([10, -10, 5, -5, 0])
    a = np.random.permutation(np.resize(levels, k // 512 * 4)).reshape(k // 512, 4)
    idx = np.arange(k)
    return np.exp2(a[idx // 512, idx % 128 // 32])


BF16 = ml_dtypes.bfloat16


def bf(x):
    return np.asarray(x, np.float32).astype(BF16)


def f64(x):
    return np.asarray(x).astype(np.float64)


B, N, D, H = 2, 128, 256, 16384


def hidden_draw():
    v = np.random.standard_normal((B, N, H)) * 1.3
    return v / (1.0 + np.exp(-1.702 * v))


def setup_inputs():
    t = mx_kscale(H)
    u = mx_kscale(D + D)
    return {"gv": bf(hidden_draw() * t),
            "ga": bf(hidden_draw() * t),
            "Wmv": bf(np.random.standard_normal((H, D)) / np.sqrt(H) / t[:, None] * u[:D]),
            "bmv": bf(np.random.standard_normal(D) * 0.3 * u[:D]),
            "Wma": bf(np.random.standard_normal((H, D)) / np.sqrt(H) / t[:, None] * u[D:]),
            "bma": bf(np.random.standard_normal(D) * 0.3 * u[D:]),
            "Wout": bf(np.random.standard_normal((D + D, D)) / np.sqrt(D + D) / u[:, None]),
            "bout": bf(np.random.standard_normal(D) * 0.3)}


def reference(gv, ga, Wmv, bmv, Wma, bma, Wout, bout):
    hv = (mxq(f64(gv), 2, "e4m3") @ mxq(f64(Wmv), 0, "e4m3")) + f64(bmv)
    ha = (mxq(f64(ga), 2, "e4m3") @ mxq(f64(Wma), 0, "e4m3")) + f64(bma)
    combined = np.concatenate([hv, ha], axis=-1)
    return (mxq(combined, 2, "e4m3") @ mxq(f64(Wout), 0, "e4m3")) + f64(bout)

@@ -1,0 +1,217 @@
+from contextlib import ExitStack
+
+import concourse.masks as masks
+import concourse.mybir as mybir
+
+BF16 = mybir.dt.bfloat16
+F32 = mybir.dt.float32
+U32 = mybir.dt.uint32
+U8 = mybir.dt.uint8
+FP8X4 = mybir.dt.float8_e4m3fn_x4
+ADD = mybir.AluOpType.add
+IDENTITY = mybir.ActivationFunctionType.Identity
+
+P = 128
+PACK = 4
+PAIR = 2
+HALVES = PACK // PAIR
+K_PASS = P * PACK
+BATCH = 2
+TOKENS = BATCH * P
+HIDDEN = 16384
+FEATURES = 256
+FEATURE_TILES = FEATURES // P
+STREAMS = 2
+PASSES = 4
+K_STEP = PASSES * K_PASS
+STEPS_PER_STREAM = HIDDEN // K_STEP
+STEPS = STREAMS * STEPS_PER_STREAM
+QUANT_PASSES = 2
+RUN = 4
+RAW_BUFS = 6
+
+FLOPS = 2 * TOKENS * FEATURES * (STREAMS * HIDDEN + STREAMS * FEATURES)
+
+
+def tile_distancefusionblock_pb_k_kernel(tc, gv, ga, Wmv, bmv, Wma, bma, Wout, bout, out):
+    nc = tc.nc
+    hidden = (gv, ga)
+    weights = (Wmv, Wma)
+
+    with ExitStack() as ctx:
+        consts = ctx.enter_context(tc.tile_pool(name="consts", bufs=1))
+        raw = ctx.enter_context(tc.tile_pool(name="raw", bufs=RAW_BUFS))
+        grouped = ctx.enter_context(tc.tile_pool(name="grouped", bufs=2))
+        quantised = ctx.enter_context(tc.tile_pool(name="quantised", bufs=3))
+        results = ctx.enter_context(tc.tile_pool(name="results", bufs=BATCH))
+        transposed = ctx.enter_context(tc.psum_pool(name="transposed", bufs=4))
+        sum_pool = ctx.enter_context(tc.psum_pool(name="sums", bufs=1))
+        small_psum = ctx.enter_context(tc.psum_pool(name="small", bufs=2))
+        ctx.enter_context(tc.manual_schedule())
+
+        raw_tiles = {}
+        operands = {}
+
+        def load(step):
+            stream, part = divmod(step, STEPS_PER_STREAM)
+            k_rows = slice(part * K_STEP, (part + 1) * K_STEP)
+            g_raw = raw.tile([P, BATCH, K_STEP], BF16)
+            nc.sync.dma_start(out=g_raw[:], in_=hidden[stream][:, :, k_rows].rearrange("b r k -> r b k"))
+            w_raw = raw.tile([P, PASSES, PACK, FEATURES], BF16)
+            nc.sync.dma_start(
+                out=w_raw[:].rearrange("p j (u e) n -> p (j u) (e n)", u=HALVES, e=PAIR),
+                in_=weights[stream][k_rows, :].rearrange(
+                    "(j u p e) n -> p (j u) (e n)", j=PASSES, u=HALVES, p=P, e=PAIR
+                ),
+            )
+            raw_tiles[step] = (g_raw, w_raw)
+
+        def quantise(values, codes, scales):
+            for first in range(0, PASSES, QUANT_PASSES):
+                some = slice(first, first + QUANT_PASSES)
+                nc.vector.quantize_mx(
+                    out=codes[:, some, :].rearrange("p j w -> p (j w)").bitcast(FP8X4),
+                    scales=scales[:, some, :].rearrange("p j w -> p (j w)"),
+                    in_=values[:, some, :].rearrange("p j v -> p (j v)"),
+                )
+
+        def prepare(step):
+            g_raw, w_raw = raw_tiles[step]
+
+            g_grouped = grouped.tile([P, PASSES, TOKENS * PACK], BF16, align_bytes=64)
+            for j in range(PASSES):
+                words = transposed.tile([P, BATCH, HALVES, P], F32)
+                for b in range(BATCH):
+                    g_words = g_raw[:, b, :].bitcast(F32)
+                    for u in range(HALVES):
+                        first = (j * HALVES + u) * P
+                        nc.tensor.transpose(words[:, b, u, :], g_words[:, first : first + P], identity[:])
+                nc.scalar.copy(
+                    out=g_grouped[:, j, :].bitcast(F32).rearrange("p (b r u) -> p b r u", b=BATCH, u=HALVES),
+                    in_=words[:].rearrange("p b u r -> p b r u"),
+                )
+            g_codes = quantised.tile([P, PASSES, TOKENS], U32, align_bytes=64)
+            g_scales = quantised.tile([P, PASSES, TOKENS], U8, align_bytes=64)
+            quantise(g_grouped, g_codes, g_scales)
+
+            w_grouped = grouped.tile([P, PASSES, FEATURES * PACK], BF16, align_bytes=64)
+            for j in range(PASSES):
+                dst = w_grouped[:, j, :].rearrange("p (c i t) -> p c t i", i=RUN, t=PACK)
+                src = w_raw[:, j, :, :].rearrange("p t (c i) -> p c t i", i=RUN)
+                if j == PASSES - 1:
+                    nc.scalar.copy(out=dst, in_=src)
+                else:
+                    nc.vector.tensor_copy(out=dst, in_=src)
+            w_codes = quantised.tile([P, PASSES, FEATURES], U32, align_bytes=64)
+            w_scales = quantised.tile([P, PASSES, FEATURES], U8, align_bytes=64)
+            quantise(w_grouped, w_codes, w_scales)
+            operands[step] = (g_codes, g_scales, w_codes, w_scales)
+
+        def multiply(step, sums):
+            g_codes, g_scales, w_codes, w_scales = operands[step]
+            part = step % STEPS_PER_STREAM
+            for j in range(PASSES):
+                for f in range(FEATURE_TILES):
+                    columns = slice(f * P, (f + 1) * P)
+                    nc.tensor.matmul_mx(
+                        out=sums[f][:],
+                        lhsT=w_codes[:, j, columns].bitcast(FP8X4),
+                        lhsT_scale=w_scales[:, j, columns],
+                        rhs=g_codes[:, j, :].bitcast(FP8X4),
+                        rhs_scale=g_scales[:, j, :],
+                        start=(part == 0 and j == 0),
+                        stop=(part == STEPS_PER_STREAM - 1 and j == PASSES - 1),
+                    )
+
+        for step in range(RAW_BUFS):
+            load(step)
+
+        identity = consts.tile([P, P], F32)
+        masks.make_identity(nc, identity[:])
+
+        bias_rows = consts.tile([P, P], BF16)
+        nc.vector.memset(bias_rows[:], 0.0)
+        bout_padded = consts.tile([P, FEATURES], BF16)
+        nc.vector.memset(bout_padded[:], 0.0)
+        ones = consts.tile([P, P], BF16)
+        nc.vector.memset(ones[:], 1.0)
+        nc.scalar.dma_start(out=bias_rows[0:FEATURE_TILES, :], in_=bmv.rearrange("(f p) -> f p", p=P))
+        nc.scalar.dma_start(
+            out=bias_rows[FEATURE_TILES : 2 * FEATURE_TILES, :], in_=bma.rearrange("(f p) -> f p", p=P)
+        )
+        nc.scalar.dma_start(out=bout_padded[0:1, :], in_=bout.rearrange("(o n) -> o n", o=1))
+        wout_raw = consts.tile([P, PACK, FEATURES], BF16)
+        nc.scalar.dma_start(out=wout_raw[:], in_=Wout.rearrange("(t p) n -> p t n", p=P))
+
+        bias_rows_f32 = consts.tile([P, P], F32)
+        nc.vector.tensor_copy(out=bias_rows_f32[:], in_=bias_rows[:])
+        bias_t = small_psum.tile([P, P], F32, tag="small")
+        nc.tensor.transpose(bias_t[:], bias_rows_f32[:], identity[:])
+        bias_cols = consts.tile([P, PACK], F32)
+        nc.vector.tensor_copy(out=bias_cols[:], in_=bias_t[:, 0:PACK])
+
+        bout_psum = small_psum.tile([P, FEATURES], F32, tag="small")
+        nc.tensor.matmul(bout_psum[:], lhsT=ones[:], rhs=bout_padded[:], start=True, stop=True)
+        bout_rows = consts.tile([P, FEATURES], F32)
+        nc.vector.tensor_copy(out=bout_rows[:], in_=bout_psum[:])
+
+        wout_grouped = consts.tile([P, FEATURES, PACK], BF16, align_bytes=64)
+        nc.vector.tensor_copy(out=wout_grouped[:], in_=wout_raw[:].rearrange("p t n -> p n t"))
+        wout_codes = consts.tile([P, FEATURES], U32, align_bytes=64)
+        wout_scales = consts.tile([P, FEATURES], U8, align_bytes=64)
+        nc.vector.quantize_mx(
+            out=wout_codes[:].bitcast(FP8X4),
+            scales=wout_scales[:],
+            in_=wout_grouped[:].rearrange("p n t -> p (n t)"),
+        )
+
+        joined = consts.tile([P, PACK, TOKENS], BF16)
+        prepare(0)
+        load(RAW_BUFS)
+        sums = None
+        for step in range(STEPS):
+            stream, part = divmod(step, STEPS_PER_STREAM)
+            if step + 1 < STEPS:
+                prepare(step + 1)
+            if step + 1 + RAW_BUFS < STEPS:
+                load(step + 1 + RAW_BUFS)
+            if part == 0:
+                sums = [sum_pool.tile([P, TOKENS], F32, name="sum%d" % f) for f in range(FEATURE_TILES)]
+            multiply(step, sums)
+            if part == STEPS_PER_STREAM - 1:
+                t = stream * FEATURE_TILES
+                nc.scalar.activation(
+                    out=joined[:, t, :], in_=sums[0][:], func=IDENTITY, bias=bias_cols[:, t : t + 1]
+                )
+                nc.vector.tensor_scalar(
+                    out=joined[:, t + 1, :],
+                    in0=sums[1][:],
+                    scalar1=bias_cols[:, t + 1 : t + 2],
+                    scalar2=None,
+                    op0=ADD,
+                )
+
+        joined_grouped = consts.tile([P, TOKENS, PACK], BF16, align_bytes=64)
+        nc.vector.tensor_copy(out=joined_grouped[:], in_=joined[:].rearrange("p t w -> p w t"))
+        joined_codes = consts.tile([P, TOKENS], U32, align_bytes=64)
+        joined_scales = consts.tile([P, TOKENS], U8, align_bytes=64)
+        nc.vector.quantize_mx(
+            out=joined_codes[:].bitcast(FP8X4),
+            scales=joined_scales[:],
+            in_=joined_grouped[:].rearrange("p w t -> p (w t)"),
+        )
+        for b in range(BATCH):
+            rows = slice(b * P, (b + 1) * P)
+            fused = small_psum.tile([P, FEATURES], F32, tag="small")
+            nc.tensor.matmul_mx(
+                out=fused[:],
+                lhsT=joined_codes[:, rows].bitcast(FP8X4),
+                lhsT_scale=joined_scales[:, rows],
+                rhs=wout_codes[:].bitcast(FP8X4),
+                rhs_scale=wout_scales[:],
+                start=True,
+                stop=True,
+            )
+            result = results.tile([P, FEATURES], F32)
+            nc.vector.tensor_tensor(out=result[:], in0=fused[:], in1=bout_rows[:], op=ADD)
+            nc.sync.dma_start(out=out[b], in_=result[:])

@@ -29,6 +29,7 @@ STEPS = STREAMS * STEPS_PER_STREAM
 QUANT_PASSES = 2
 RUN = 4
 RAW_BUFS = 6
+VECTOR_COLUMNS = PASSES * FEATURES * 5 // 8
 
 FLOPS = 2 * TOKENS * FEATURES * (STREAMS * HIDDEN + STREAMS * FEATURES)
 
@@ -41,7 +42,7 @@ def tile_distancefusionblock_pb_k_kernel(tc, gv, ga, Wmv, bmv, Wma, bma, Wout, b
     with ExitStack() as ctx:
         consts = ctx.enter_context(tc.tile_pool(name="consts", bufs=1))
         raw = ctx.enter_context(tc.tile_pool(name="raw", bufs=RAW_BUFS))
-        grouped = ctx.enter_context(tc.tile_pool(name="grouped", bufs=2))
+        grouped = ctx.enter_context(tc.tile_pool(name="grouped", bufs=3))
         quantised = ctx.enter_context(tc.tile_pool(name="quantised", bufs=3))
         results = ctx.enter_context(tc.tile_pool(name="results", bufs=BATCH))
         transposed = ctx.enter_context(tc.psum_pool(name="transposed", bufs=4))
@@ -90,18 +91,20 @@ def tile_distancefusionblock_pb_k_kernel(tc, gv, ga, Wmv, bmv, Wma, bma, Wout, b
                     out=g_grouped[:, j, :].bitcast(F32).rearrange("p (b r u) -> p b r u", b=BATCH, u=HALVES),
                     in_=words[:].rearrange("p b u r -> p b r u"),
                 )
-            g_codes = quantised.tile([P, PASSES, TOKENS], U32, align_bytes=64)
-            g_scales = quantised.tile([P, PASSES, TOKENS], U8, align_bytes=64)
-            quantise(g_grouped, g_codes, g_scales)
 
             w_grouped = grouped.tile([P, PASSES, FEATURES * PACK], BF16, align_bytes=64)
             for j in range(PASSES):
                 dst = w_grouped[:, j, :].rearrange("p (c i t) -> p c t i", i=RUN, t=PACK)
                 src = w_raw[:, j, :, :].rearrange("p t (c i) -> p c t i", i=RUN)
-                if j == PASSES - 1:
-                    nc.scalar.copy(out=dst, in_=src)
-                else:
-                    nc.vector.tensor_copy(out=dst, in_=src)
+                cut = min(max(VECTOR_COLUMNS - j * FEATURES, 0), FEATURES) // RUN
+                if cut > 0:
+                    nc.vector.tensor_copy(out=dst[:, :cut], in_=src[:, :cut])
+                if cut < FEATURES // RUN:
+                    nc.scalar.copy(out=dst[:, cut:], in_=src[:, cut:])
+
+            g_codes = quantised.tile([P, PASSES, TOKENS], U32, align_bytes=64)
+            g_scales = quantised.tile([P, PASSES, TOKENS], U8, align_bytes=64)
+            quantise(g_grouped, g_codes, g_scales)
             w_codes = quantised.tile([P, PASSES, FEATURES], U32, align_bytes=64)
             w_scales = quantised.tile([P, PASSES, FEATURES], U8, align_bytes=64)
             quantise(w_grouped, w_codes, w_scales)
@@ -123,9 +126,6 @@ def tile_distancefusionblock_pb_k_kernel(tc, gv, ga, Wmv, bmv, Wma, bma, Wout, b
                         stop=(part == STEPS_PER_STREAM - 1 and j == PASSES - 1),
                     )
 
-        for step in range(RAW_BUFS):
-            load(step)
-
         identity = consts.tile([P, P], F32)
         masks.make_identity(nc, identity[:])
 
@@ -142,6 +142,10 @@ def tile_distancefusionblock_pb_k_kernel(tc, gv, ga, Wmv, bmv, Wma, bma, Wout, b
         nc.scalar.dma_start(out=bout_padded[0:1, :], in_=bout.rearrange("(o n) -> o n", o=1))
         wout_raw = consts.tile([P, PACK, FEATURES], BF16)
         nc.scalar.dma_start(out=wout_raw[:], in_=Wout.rearrange("(t p) n -> p t n", p=P))
+        for step in range(RAW_BUFS):
+            load(step)
+        prepare(0)
+        load(RAW_BUFS)
 
         bias_rows_f32 = consts.tile([P, P], F32)
         nc.vector.tensor_copy(out=bias_rows_f32[:], in_=bias_rows[:])
@@ -166,8 +170,6 @@ def tile_distancefusionblock_pb_k_kernel(tc, gv, ga, Wmv, bmv, Wma, bma, Wout, b
         )
 
         joined = consts.tile([P, PACK, TOKENS], BF16)
-        prepare(0)
-        load(RAW_BUFS)
         sums = None
         for step in range(STEPS):
             stream, part = divmod(step, STEPS_PER_STREAM)

@@ -60,10 +60,8 @@ def tile_distancefusionblock_pb_k_kernel(tc, gv, ga, Wmv, bmv, Wma, bma, Wout, b
             nc.sync.dma_start(out=g_raw[:], in_=hidden[stream][:, :, k_rows].rearrange("b r k -> r b k"))
             w_raw = raw.tile([P, PASSES, PACK, FEATURES], BF16)
             nc.sync.dma_start(
-                out=w_raw[:].rearrange("p j (u e) n -> p (j u) (e n)", u=HALVES, e=PAIR),
-                in_=weights[stream][k_rows, :].rearrange(
-                    "(j u p e) n -> p (j u) (e n)", j=PASSES, u=HALVES, p=P, e=PAIR
-                ),
+                out=w_raw[:].rearrange("p j t n -> p j (t n)"),
+                in_=weights[stream][k_rows, :].rearrange("(j p t) n -> p j (t n)", j=PASSES, p=P, t=PACK),
             )
             raw_tiles[step] = (g_raw, w_raw)
 
@@ -83,10 +81,9 @@ def tile_distancefusionblock_pb_k_kernel(tc, gv, ga, Wmv, bmv, Wma, bma, Wout, b
             for j in range(PASSES):
                 words = transposed.tile([P, BATCH, HALVES, P], F32)
                 for b in range(BATCH):
-                    g_words = g_raw[:, b, :].bitcast(F32)
+                    g_words = g_raw[:, b, :].bitcast(F32).rearrange("r (j p u) -> r j u p", j=PASSES, u=HALVES)
                     for u in range(HALVES):
-                        first = (j * HALVES + u) * P
-                        nc.tensor.transpose(words[:, b, u, :], g_words[:, first : first + P], identity[:])
+                        nc.tensor.transpose(words[:, b, u, :], g_words[:, j, u, :], identity[:])
                 nc.scalar.copy(
                     out=g_grouped[:, j, :].bitcast(F32).rearrange("p (b r u) -> p b r u", b=BATCH, u=HALVES),
                     in_=words[:].rearrange("p b u r -> p b r u"),

@@ -23,13 +23,30 @@ FEATURES = 256
 FEATURE_TILES = FEATURES // P
 STREAMS = 2
 PASSES = 4
-K_STEP = PASSES * K_PASS
-STEPS_PER_STREAM = HIDDEN // K_STEP
-STEPS = STREAMS * STEPS_PER_STREAM
+K_BLOCK = PASSES * K_PASS
+BLOCKS_PER_STREAM = HIDDEN // K_BLOCK
+LAST_BLOCK_STEPS = (2, 1, 1)
 QUANT_PASSES = 2
+PE_RUN = 2
 RUN = 4
 RAW_BUFS = 6
-VECTOR_COLUMNS = PASSES * FEATURES * 5 // 8
+def vector_columns(passes):
+    return passes * FEATURES * 5 // 8
+
+
+def list_steps():
+    steps = []
+    for stream in range(STREAMS):
+        for block in range(BLOCKS_PER_STREAM):
+            is_last = stream == STREAMS - 1 and block == BLOCKS_PER_STREAM - 1
+            first = 0
+            for passes in LAST_BLOCK_STEPS if is_last else (PASSES,):
+                steps.append((stream, block, first, passes))
+                first += passes
+    return steps
+
+
+STEPS = list_steps()
 
 FLOPS = 2 * TOKENS * FEATURES * (STREAMS * HIDDEN + STREAMS * FEATURES)
 
@@ -51,32 +68,37 @@ def tile_distancefusionblock_pb_k_kernel(tc, gv, ga, Wmv, bmv, Wma, bma, Wout, b
         ctx.enter_context(tc.manual_schedule())
 
         raw_tiles = {}
+        block_operands = {}
         operands = {}
 
         def load(step):
-            stream, part = divmod(step, STEPS_PER_STREAM)
-            k_rows = slice(part * K_STEP, (part + 1) * K_STEP)
-            g_raw = raw.tile([P, BATCH, K_STEP], BF16)
-            nc.sync.dma_start(out=g_raw[:], in_=hidden[stream][:, :, k_rows].rearrange("b r k -> r b k"))
-            w_raw = raw.tile([P, PASSES, PACK, FEATURES], BF16)
+            stream, block, first, passes = STEPS[step]
+            if first == 0:
+                k_rows = slice(block * K_BLOCK, (block + 1) * K_BLOCK)
+                g_raw = raw.tile([P, BATCH, K_BLOCK], BF16)
+                nc.sync.dma_start(out=g_raw[:], in_=hidden[stream][:, :, k_rows].rearrange("b r k -> r b k"))
+                raw_tiles["g", stream, block] = g_raw
+            k_first = block * K_BLOCK + first * K_PASS
+            w_raw = raw.tile([P, passes, PACK, FEATURES], BF16)
             nc.sync.dma_start(
                 out=w_raw[:].rearrange("p j t n -> p j (t n)"),
-                in_=weights[stream][k_rows, :].rearrange("(j p t) n -> p j (t n)", j=PASSES, p=P, t=PACK),
+                in_=weights[stream][k_first : k_first + passes * K_PASS, :].rearrange(
+                    "(j p t) n -> p j (t n)", j=passes, p=P, t=PACK
+                ),
             )
-            raw_tiles[step] = (g_raw, w_raw)
+            raw_tiles["w", step] = w_raw
 
-        def quantise(values, codes, scales):
-            for first in range(0, PASSES, QUANT_PASSES):
-                some = slice(first, first + QUANT_PASSES)
+        def quantise(values, codes, scales, passes):
+            for first in range(0, passes, QUANT_PASSES):
+                some = slice(first, min(first + QUANT_PASSES, passes))
                 nc.vector.quantize_mx(
                     out=codes[:, some, :].rearrange("p j w -> p (j w)").bitcast(FP8X4),
                     scales=scales[:, some, :].rearrange("p j w -> p (j w)"),
                     in_=values[:, some, :].rearrange("p j v -> p (j v)"),
                 )
 
-        def prepare(step):
-            g_raw, w_raw = raw_tiles[step]
-
+        def transpose(stream, block, between):
+            g_raw = raw_tiles["g", stream, block]
             g_grouped = grouped.tile([P, PASSES, TOKENS * PACK], BF16, align_bytes=64)
             for j in range(PASSES):
                 words = transposed.tile([P, BATCH, HALVES, P], F32)
@@ -88,39 +110,54 @@ def tile_distancefusionblock_pb_k_kernel(tc, gv, ga, Wmv, bmv, Wma, bma, Wout, b
                     out=g_grouped[:, j, :].bitcast(F32).rearrange("p (b r u) -> p b r u", b=BATCH, u=HALVES),
                     in_=words[:].rearrange("p b u r -> p b r u"),
                 )
+                if (j + 1) % PE_RUN == 0:
+                    between()
+            return g_grouped
 
-            w_grouped = grouped.tile([P, PASSES, FEATURES * PACK], BF16, align_bytes=64)
-            for j in range(PASSES):
+        def regroup(step):
+            passes = STEPS[step][3]
+            w_raw = raw_tiles["w", step]
+            w_grouped = grouped.tile([P, passes, FEATURES * PACK], BF16, align_bytes=64)
+            for j in range(passes):
                 dst = w_grouped[:, j, :].rearrange("p (c i t) -> p c t i", i=RUN, t=PACK)
                 src = w_raw[:, j, :, :].rearrange("p t (c i) -> p c t i", i=RUN)
-                cut = min(max(VECTOR_COLUMNS - j * FEATURES, 0), FEATURES) // RUN
+                cut = min(max(vector_columns(passes) - j * FEATURES, 0), FEATURES) // RUN
                 if cut > 0:
                     nc.vector.tensor_copy(out=dst[:, :cut], in_=src[:, :cut])
                 if cut < FEATURES // RUN:
                     nc.scalar.copy(out=dst[:, cut:], in_=src[:, cut:])
+            return w_grouped
 
-            g_codes = quantised.tile([P, PASSES, TOKENS], U32, align_bytes=64)
-            g_scales = quantised.tile([P, PASSES, TOKENS], U8, align_bytes=64)
-            quantise(g_grouped, g_codes, g_scales)
-            w_codes = quantised.tile([P, PASSES, FEATURES], U32, align_bytes=64)
-            w_scales = quantised.tile([P, PASSES, FEATURES], U8, align_bytes=64)
-            quantise(w_grouped, w_codes, w_scales)
-            operands[step] = (g_codes, g_scales, w_codes, w_scales)
+        def prepare(step, between):
+            stream, block, first, passes = STEPS[step]
+            if first == 0:
+                g_grouped = transpose(stream, block, between)
+            w_grouped = regroup(step)
+            if first == 0:
+                g_codes = quantised.tile([P, PASSES, TOKENS], U32, align_bytes=64)
+                g_scales = quantised.tile([P, PASSES, TOKENS], U8, align_bytes=64)
+                quantise(g_grouped, g_codes, g_scales, PASSES)
+                block_operands[stream, block] = (g_codes, g_scales)
+            w_codes = quantised.tile([P, passes, FEATURES], U32, align_bytes=64)
+            w_scales = quantised.tile([P, passes, FEATURES], U8, align_bytes=64)
+            quantise(w_grouped, w_codes, w_scales, passes)
+            operands[step] = (w_codes, w_scales)
 
-        def multiply(step, sums):
-            g_codes, g_scales, w_codes, w_scales = operands[step]
-            part = step % STEPS_PER_STREAM
-            for j in range(PASSES):
+        def multiply(step, which, sums):
+            stream, block, first, passes = STEPS[step]
+            g_codes, g_scales = block_operands[stream, block]
+            w_codes, w_scales = operands[step]
+            for j in which:
                 for f in range(FEATURE_TILES):
                     columns = slice(f * P, (f + 1) * P)
                     nc.tensor.matmul_mx(
                         out=sums[f][:],
                         lhsT=w_codes[:, j, columns].bitcast(FP8X4),
                         lhsT_scale=w_scales[:, j, columns],
-                        rhs=g_codes[:, j, :].bitcast(FP8X4),
-                        rhs_scale=g_scales[:, j, :],
-                        start=(part == 0 and j == 0),
-                        stop=(part == STEPS_PER_STREAM - 1 and j == PASSES - 1),
+                        rhs=g_codes[:, first + j, :].bitcast(FP8X4),
+                        rhs_scale=g_scales[:, first + j, :],
+                        start=(block == 0 and first + j == 0),
+                        stop=(block == BLOCKS_PER_STREAM - 1 and first + j == PASSES - 1),
                     )
 
         identity = consts.tile([P, P], F32)
@@ -141,7 +178,7 @@ def tile_distancefusionblock_pb_k_kernel(tc, gv, ga, Wmv, bmv, Wma, bma, Wout, b
         nc.scalar.dma_start(out=wout_raw[:], in_=Wout.rearrange("(t p) n -> p t n", p=P))
         for step in range(RAW_BUFS):
             load(step)
-        prepare(0)
+        prepare(0, lambda: None)
         load(RAW_BUFS)
 
         bias_rows_f32 = consts.tile([P, P], F32)
@@ -168,16 +205,22 @@ def tile_distancefusionblock_pb_k_kernel(tc, gv, ga, Wmv, bmv, Wma, bma, Wout, b
 
         joined = consts.tile([P, PACK, TOKENS], BF16)
         sums = None
-        for step in range(STEPS):
-            stream, part = divmod(step, STEPS_PER_STREAM)
-            if step + 1 < STEPS:
-                prepare(step + 1)
-            if step + 1 + RAW_BUFS < STEPS:
-                load(step + 1 + RAW_BUFS)
-            if part == 0:
+        for step in range(len(STEPS)):
+            stream, block, first, passes = STEPS[step]
+            if block == 0:
                 sums = [sum_pool.tile([P, TOKENS], F32, name="sum%d" % f) for f in range(FEATURE_TILES)]
-            multiply(step, sums)
-            if part == STEPS_PER_STREAM - 1:
+            left = list(range(passes))
+
+            def some_passes():
+                multiply(step, left[:PE_RUN], sums)
+                left[:] = left[PE_RUN:]
+
+            if step + 1 < len(STEPS):
+                prepare(step + 1, some_passes)
+            if step + 1 + RAW_BUFS < len(STEPS):
+                load(step + 1 + RAW_BUFS)
+            multiply(step, left, sums)
+            if block == BLOCKS_PER_STREAM - 1 and first + passes == PASSES:
                 t = stream * FEATURE_TILES
                 nc.scalar.activation(
                     out=joined[:, t, :], in_=sums[0][:], func=IDENTITY, bias=bias_cols[:, t : t + 1]

@@ -60,11 +60,10 @@ def tile_distancefusionblock_pb_k_kernel(tc, gv, ga, Wmv, bmv, Wma, bma, Wout, b
         consts = ctx.enter_context(tc.tile_pool(name="consts", bufs=1))
         raw = ctx.enter_context(tc.tile_pool(name="raw", bufs=RAW_BUFS))
         grouped = ctx.enter_context(tc.tile_pool(name="grouped", bufs=3))
-        quantised = ctx.enter_context(tc.tile_pool(name="quantised", bufs=3))
+        quantised = ctx.enter_context(tc.tile_pool(name="quantised", bufs=4))
         results = ctx.enter_context(tc.tile_pool(name="results", bufs=BATCH))
         transposed = ctx.enter_context(tc.psum_pool(name="transposed", bufs=4))
-        sum_pool = ctx.enter_context(tc.psum_pool(name="sums", bufs=1))
-        small_psum = ctx.enter_context(tc.psum_pool(name="small", bufs=2))
+        banks = ctx.enter_context(tc.psum_pool(name="banks", bufs=1))
         ctx.enter_context(tc.manual_schedule())
 
         raw_tiles = {}
@@ -143,22 +142,26 @@ def tile_distancefusionblock_pb_k_kernel(tc, gv, ga, Wmv, bmv, Wma, bma, Wout, b
             quantise(w_grouped, w_codes, w_scales, passes)
             operands[step] = (w_codes, w_scales)
 
-        def multiply(step, which, sums):
+        sums = {}
+
+        def multiply(step, j):
             stream, block, first, passes = STEPS[step]
             g_codes, g_scales = block_operands[stream, block]
             w_codes, w_scales = operands[step]
-            for j in which:
+            if block == 0 and first + j == 0:
                 for f in range(FEATURE_TILES):
-                    columns = slice(f * P, (f + 1) * P)
-                    nc.tensor.matmul_mx(
-                        out=sums[f][:],
-                        lhsT=w_codes[:, j, columns].bitcast(FP8X4),
-                        lhsT_scale=w_scales[:, j, columns],
-                        rhs=g_codes[:, first + j, :].bitcast(FP8X4),
-                        rhs_scale=g_scales[:, first + j, :],
-                        start=(block == 0 and first + j == 0),
-                        stop=(block == BLOCKS_PER_STREAM - 1 and first + j == PASSES - 1),
-                    )
+                    sums[stream, f] = banks.tile([P, TOKENS], F32, name="sum", tag="sum%d_%d" % (stream, f))
+            for f in range(FEATURE_TILES):
+                columns = slice(f * P, (f + 1) * P)
+                nc.tensor.matmul_mx(
+                    out=sums[stream, f][:],
+                    lhsT=w_codes[:, j, columns].bitcast(FP8X4),
+                    lhsT_scale=w_scales[:, j, columns],
+                    rhs=g_codes[:, first + j, :].bitcast(FP8X4),
+                    rhs_scale=g_scales[:, first + j, :],
+                    start=(block == 0 and first + j == 0),
+                    stop=(block == BLOCKS_PER_STREAM - 1 and first + j == PASSES - 1),
+                )
 
         identity = consts.tile([P, P], F32)
         masks.make_identity(nc, identity[:])
@@ -178,17 +181,17 @@ def tile_distancefusionblock_pb_k_kernel(tc, gv, ga, Wmv, bmv, Wma, bma, Wout, b
         nc.scalar.dma_start(out=wout_raw[:], in_=Wout.rearrange("(t p) n -> p t n", p=P))
         for step in range(RAW_BUFS):
             load(step)
-        prepare(0, lambda: None)
+        prepare(0, list)
         load(RAW_BUFS)
 
         bias_rows_f32 = consts.tile([P, P], F32)
         nc.vector.tensor_copy(out=bias_rows_f32[:], in_=bias_rows[:])
-        bias_t = small_psum.tile([P, P], F32, tag="small")
+        bias_t = banks.tile([P, P], F32, tag="sum1_0")
         nc.tensor.transpose(bias_t[:], bias_rows_f32[:], identity[:])
         bias_cols = consts.tile([P, PACK], F32)
         nc.vector.tensor_copy(out=bias_cols[:], in_=bias_t[:, 0:PACK])
 
-        bout_psum = small_psum.tile([P, FEATURES], F32, tag="small")
+        bout_psum = banks.tile([P, FEATURES], F32, tag="sum1_1")
         nc.tensor.matmul(bout_psum[:], lhsT=ones[:], rhs=bout_padded[:], start=True, stop=True)
         bout_rows = consts.tile([P, FEATURES], F32)
         nc.vector.tensor_copy(out=bout_rows[:], in_=bout_psum[:])
@@ -204,34 +207,39 @@ def tile_distancefusionblock_pb_k_kernel(tc, gv, ga, Wmv, bmv, Wma, bma, Wout, b
         )
 
         joined = consts.tile([P, PACK, TOKENS], BF16)
-        sums = None
+
+        def leave(stream):
+            t = stream * FEATURE_TILES
+            nc.scalar.activation(
+                out=joined[:, t, :], in_=sums[stream, 0][:], func=IDENTITY, bias=bias_cols[:, t : t + 1]
+            )
+            nc.vector.tensor_scalar(
+                out=joined[:, t + 1, :],
+                in0=sums[stream, 1][:],
+                scalar1=bias_cols[:, t + 1 : t + 2],
+                scalar2=None,
+                op0=ADD,
+            )
+
+        waiting = []
+
+        def some_passes():
+            for step, j in waiting[:PE_RUN]:
+                multiply(step, j)
+            waiting[:] = waiting[PE_RUN:]
+
         for step in range(len(STEPS)):
-            stream, block, first, passes = STEPS[step]
-            if block == 0:
-                sums = [sum_pool.tile([P, TOKENS], F32, name="sum%d" % f) for f in range(FEATURE_TILES)]
-            left = list(range(passes))
-
-            def some_passes():
-                multiply(step, left[:PE_RUN], sums)
-                left[:] = left[PE_RUN:]
-
             if step + 1 < len(STEPS):
                 prepare(step + 1, some_passes)
             if step + 1 + RAW_BUFS < len(STEPS):
                 load(step + 1 + RAW_BUFS)
-            multiply(step, left, sums)
-            if block == BLOCKS_PER_STREAM - 1 and first + passes == PASSES:
-                t = stream * FEATURE_TILES
-                nc.scalar.activation(
-                    out=joined[:, t, :], in_=sums[0][:], func=IDENTITY, bias=bias_cols[:, t : t + 1]
-                )
-                nc.vector.tensor_scalar(
-                    out=joined[:, t + 1, :],
-                    in0=sums[1][:],
-                    scalar1=bias_cols[:, t + 1 : t + 2],
-                    scalar2=None,
-                    op0=ADD,
-                )
+            if step >= 2 and STEPS[step - 2][:2] == (0, BLOCKS_PER_STREAM - 1):
+                leave(0)
+            waiting += [(step, j) for j in range(STEPS[step][3])]
+            if step + 2 >= len(STEPS) or STEPS[step + 2][2] > 0:
+                while waiting:
+                    some_passes()
+        leave(1)
 
         joined_grouped = consts.tile([P, TOKENS, PACK], BF16, align_bytes=64)
         nc.vector.tensor_copy(out=joined_grouped[:], in_=joined[:].rearrange("p t w -> p w t"))
@@ -244,7 +252,7 @@ def tile_distancefusionblock_pb_k_kernel(tc, gv, ga, Wmv, bmv, Wma, bma, Wout, b
         )
         for b in range(BATCH):
             rows = slice(b * P, (b + 1) * P)
-            fused = small_psum.tile([P, FEATURES], F32, tag="small")
+            fused = banks.tile([P, FEATURES], F32, tag="sum0_%d" % b)
             nc.tensor.matmul_mx(
                 out=fused[:],
                 lhsT=joined_codes[:, rows].bitcast(FP8X4),

@@ -22,31 +22,46 @@ HIDDEN = 16384
 FEATURES = 256
 FEATURE_TILES = FEATURES // P
 STREAMS = 2
-PASSES = 4
-K_BLOCK = PASSES * K_PASS
-BLOCKS_PER_STREAM = HIDDEN // K_BLOCK
-LAST_BLOCK_STEPS = (2, 1, 1)
+PASSES_PER_STREAM = HIDDEN // K_PASS
+BLOCK_PASSES = ((2, 2) + 7 * (4,), 7 * (4,) + (2, 1, 1))
+HIDDEN_LOADS = ((2, 2, 4, 8, 8, 8), (8, 8, 8, 4, 2, 1, 1))
 QUANT_PASSES = 2
 PE_RUN = 2
 RUN = 4
-RAW_BUFS = 6
-def vector_columns(passes):
-    return passes * FEATURES * 5 // 8
+WEIGHT_BUFS = 6
+HIDDEN_BUFS = 4
+VECTOR_COLUMNS = FEATURES * 5 // 8
 
 
-def list_steps():
-    steps = []
+def list_pieces(passes_of):
+    pieces = []
     for stream in range(STREAMS):
-        for block in range(BLOCKS_PER_STREAM):
-            is_last = stream == STREAMS - 1 and block == BLOCKS_PER_STREAM - 1
-            first = 0
-            for passes in LAST_BLOCK_STEPS if is_last else (PASSES,):
-                steps.append((stream, block, first, passes))
-                first += passes
-    return steps
+        first = 0
+        for passes in passes_of[stream]:
+            pieces.append((stream, first, passes))
+            first += passes
+        assert first == PASSES_PER_STREAM
+    return pieces
 
 
-STEPS = list_steps()
+BLOCKS = list_pieces(BLOCK_PASSES)
+HIDDEN_PIECES = list_pieces(HIDDEN_LOADS)
+
+
+def blocks_of(piece):
+    stream, first, passes = piece
+    return [i for i, (s, f, p) in enumerate(BLOCKS) if s == stream and first <= f < first + passes]
+
+
+def list_loads():
+    loads = []
+    for piece_index, piece in enumerate(HIDDEN_PIECES):
+        blocks = blocks_of(piece)
+        reused = piece_index - HIDDEN_BUFS
+        loads.append(("hidden", piece_index, blocks_of(HIDDEN_PIECES[reused])[-1] if reused >= 0 else -1))
+        for block in blocks:
+            loads.append(("weights", block, block - WEIGHT_BUFS))
+    return loads
 
 FLOPS = 2 * TOKENS * FEATURES * (STREAMS * HIDDEN + STREAMS * FEATURES)
 
@@ -58,7 +73,7 @@ def tile_distancefusionblock_pb_k_kernel(tc, gv, ga, Wmv, bmv, Wma, bma, Wout, b
 
     with ExitStack() as ctx:
         consts = ctx.enter_context(tc.tile_pool(name="consts", bufs=1))
-        raw = ctx.enter_context(tc.tile_pool(name="raw", bufs=RAW_BUFS))
+        raw = ctx.enter_context(tc.tile_pool(name="raw", bufs=1))
         grouped = ctx.enter_context(tc.tile_pool(name="grouped", bufs=3))
         quantised = ctx.enter_context(tc.tile_pool(name="quantised", bufs=4))
         results = ctx.enter_context(tc.tile_pool(name="results", bufs=BATCH))
@@ -67,88 +82,74 @@ def tile_distancefusionblock_pb_k_kernel(tc, gv, ga, Wmv, bmv, Wma, bma, Wout, b
         ctx.enter_context(tc.manual_schedule())
 
         raw_tiles = {}
-        block_operands = {}
         operands = {}
+        sums = {}
 
-        def load(step):
-            stream, block, first, passes = STEPS[step]
-            if first == 0:
-                k_rows = slice(block * K_BLOCK, (block + 1) * K_BLOCK)
-                g_raw = raw.tile([P, BATCH, K_BLOCK], BF16)
-                nc.sync.dma_start(out=g_raw[:], in_=hidden[stream][:, :, k_rows].rearrange("b r k -> r b k"))
-                raw_tiles["g", stream, block] = g_raw
-            k_first = block * K_BLOCK + first * K_PASS
-            w_raw = raw.tile([P, passes, PACK, FEATURES], BF16)
+        def load_hidden(index):
+            stream, first, passes = HIDDEN_PIECES[index]
+            k_rows = slice(first * K_PASS, (first + passes) * K_PASS)
+            g_raw = raw.tile([P, BATCH, passes * K_PASS], BF16, bufs=HIDDEN_BUFS)
+            nc.sync.dma_start(out=g_raw[:], in_=hidden[stream][:, :, k_rows].rearrange("b r k -> r b k"))
+            for block in blocks_of(HIDDEN_PIECES[index]):
+                raw_tiles["g", block] = (g_raw, BLOCKS[block][1] - first)
+
+        def load_weights(block):
+            stream, first, passes = BLOCKS[block]
+            k_rows = slice(first * K_PASS, (first + passes) * K_PASS)
+            w_raw = raw.tile([P, passes, PACK, FEATURES], BF16, bufs=WEIGHT_BUFS)
             nc.sync.dma_start(
                 out=w_raw[:].rearrange("p j t n -> p j (t n)"),
-                in_=weights[stream][k_first : k_first + passes * K_PASS, :].rearrange(
-                    "(j p t) n -> p j (t n)", j=passes, p=P, t=PACK
-                ),
+                in_=weights[stream][k_rows, :].rearrange("(j p t) n -> p j (t n)", j=passes, p=P, t=PACK),
             )
-            raw_tiles["w", step] = w_raw
+            raw_tiles["w", block] = w_raw
 
         def quantise(values, codes, scales, passes):
-            for first in range(0, passes, QUANT_PASSES):
-                some = slice(first, min(first + QUANT_PASSES, passes))
+            for j in range(0, passes, QUANT_PASSES):
+                some = slice(j, min(j + QUANT_PASSES, passes))
                 nc.vector.quantize_mx(
                     out=codes[:, some, :].rearrange("p j w -> p (j w)").bitcast(FP8X4),
                     scales=scales[:, some, :].rearrange("p j w -> p (j w)"),
                     in_=values[:, some, :].rearrange("p j v -> p (j v)"),
                 )
 
-        def transpose(stream, block, between):
-            g_raw = raw_tiles["g", stream, block]
-            g_grouped = grouped.tile([P, PASSES, TOKENS * PACK], BF16, align_bytes=64)
-            for j in range(PASSES):
+        def prepare(block, between):
+            stream, first, passes = BLOCKS[block]
+            g_raw, g_first = raw_tiles["g", block]
+            w_raw = raw_tiles["w", block]
+
+            g_grouped = grouped.tile([P, passes, TOKENS * PACK], BF16, align_bytes=64)
+            for j in range(passes):
                 words = transposed.tile([P, BATCH, HALVES, P], F32)
                 for b in range(BATCH):
-                    g_words = g_raw[:, b, :].bitcast(F32).rearrange("r (j p u) -> r j u p", j=PASSES, u=HALVES)
+                    g_words = g_raw[:, b, :].bitcast(F32).rearrange("r (j p u) -> r j u p", p=P, u=HALVES)
                     for u in range(HALVES):
-                        nc.tensor.transpose(words[:, b, u, :], g_words[:, j, u, :], identity[:])
+                        nc.tensor.transpose(words[:, b, u, :], g_words[:, g_first + j, u, :], identity[:])
                 nc.scalar.copy(
                     out=g_grouped[:, j, :].bitcast(F32).rearrange("p (b r u) -> p b r u", b=BATCH, u=HALVES),
                     in_=words[:].rearrange("p b u r -> p b r u"),
                 )
-                if (j + 1) % PE_RUN == 0:
+                if (j + 1) % PE_RUN == 0 or j == passes - 1:
                     between()
-            return g_grouped
 
-        def regroup(step):
-            passes = STEPS[step][3]
-            w_raw = raw_tiles["w", step]
             w_grouped = grouped.tile([P, passes, FEATURES * PACK], BF16, align_bytes=64)
-            for j in range(passes):
-                dst = w_grouped[:, j, :].rearrange("p (c i t) -> p c t i", i=RUN, t=PACK)
-                src = w_raw[:, j, :, :].rearrange("p t (c i) -> p c t i", i=RUN)
-                cut = min(max(vector_columns(passes) - j * FEATURES, 0), FEATURES) // RUN
-                if cut > 0:
-                    nc.vector.tensor_copy(out=dst[:, :cut], in_=src[:, :cut])
-                if cut < FEATURES // RUN:
-                    nc.scalar.copy(out=dst[:, cut:], in_=src[:, cut:])
-            return w_grouped
+            dst = w_grouped[:].rearrange("p j (c i t) -> p j c t i", i=RUN, t=PACK)
+            src = w_raw[:].rearrange("p j t (c i) -> p j c t i", i=RUN)
+            cut = VECTOR_COLUMNS // RUN
+            nc.vector.tensor_copy(out=dst[:, :, :cut], in_=src[:, :, :cut])
+            nc.scalar.copy(out=dst[:, :, cut:], in_=src[:, :, cut:])
 
-        def prepare(step, between):
-            stream, block, first, passes = STEPS[step]
-            if first == 0:
-                g_grouped = transpose(stream, block, between)
-            w_grouped = regroup(step)
-            if first == 0:
-                g_codes = quantised.tile([P, PASSES, TOKENS], U32, align_bytes=64)
-                g_scales = quantised.tile([P, PASSES, TOKENS], U8, align_bytes=64)
-                quantise(g_grouped, g_codes, g_scales, PASSES)
-                block_operands[stream, block] = (g_codes, g_scales)
+            g_codes = quantised.tile([P, passes, TOKENS], U32, align_bytes=64)
+            g_scales = quantised.tile([P, passes, TOKENS], U8, align_bytes=64)
+            quantise(g_grouped, g_codes, g_scales, passes)
             w_codes = quantised.tile([P, passes, FEATURES], U32, align_bytes=64)
             w_scales = quantised.tile([P, passes, FEATURES], U8, align_bytes=64)
             quantise(w_grouped, w_codes, w_scales, passes)
-            operands[step] = (w_codes, w_scales)
+            operands[block] = (g_codes, g_scales, w_codes, w_scales)
 
-        sums = {}
-
-        def multiply(step, j):
-            stream, block, first, passes = STEPS[step]
-            g_codes, g_scales = block_operands[stream, block]
-            w_codes, w_scales = operands[step]
-            if block == 0 and first + j == 0:
+        def multiply(block, j):
+            stream, first, passes = BLOCKS[block]
+            g_codes, g_scales, w_codes, w_scales = operands[block]
+            if first + j == 0:
                 for f in range(FEATURE_TILES):
                     sums[stream, f] = banks.tile([P, TOKENS], F32, name="sum", tag="sum%d_%d" % (stream, f))
             for f in range(FEATURE_TILES):
@@ -157,10 +158,10 @@ def tile_distancefusionblock_pb_k_kernel(tc, gv, ga, Wmv, bmv, Wma, bma, Wout, b
                     out=sums[stream, f][:],
                     lhsT=w_codes[:, j, columns].bitcast(FP8X4),
                     lhsT_scale=w_scales[:, j, columns],
-                    rhs=g_codes[:, first + j, :].bitcast(FP8X4),
-                    rhs_scale=g_scales[:, first + j, :],
-                    start=(block == 0 and first + j == 0),
-                    stop=(block == BLOCKS_PER_STREAM - 1 and first + j == PASSES - 1),
+                    rhs=g_codes[:, j, :].bitcast(FP8X4),
+                    rhs_scale=g_scales[:, j, :],
+                    start=(first + j == 0),
+                    stop=(first + j == PASSES_PER_STREAM - 1),
                 )
 
         identity = consts.tile([P, P], F32)
@@ -172,20 +173,32 @@ def tile_distancefusionblock_pb_k_kernel(tc, gv, ga, Wmv, bmv, Wma, bma, Wout, b
         nc.vector.memset(bout_padded[:], 0.0)
         ones = consts.tile([P, P], BF16)
         nc.vector.memset(ones[:], 1.0)
-        nc.scalar.dma_start(out=bias_rows[0:FEATURE_TILES, :], in_=bmv.rearrange("(f p) -> f p", p=P))
-        nc.scalar.dma_start(
+        wout_raw = consts.tile([P, PACK, FEATURES], BF16)
+        loads = list_loads()[4:]
+
+        def start_loads(prepared):
+            while loads and loads[0][2] <= prepared:
+                kind, index = loads[0][:2]
+                loads[:] = loads[1:]
+                if kind == "hidden":
+                    load_hidden(index)
+                else:
+                    load_weights(index)
+
+        load_hidden(0)
+        nc.sync.dma_start(out=bias_rows[0:FEATURE_TILES, :], in_=bmv.rearrange("(f p) -> f p", p=P))
+        nc.sync.dma_start(
             out=bias_rows[FEATURE_TILES : 2 * FEATURE_TILES, :], in_=bma.rearrange("(f p) -> f p", p=P)
         )
-        nc.scalar.dma_start(out=bout_padded[0:1, :], in_=bout.rearrange("(o n) -> o n", o=1))
-        wout_raw = consts.tile([P, PACK, FEATURES], BF16)
-        nc.scalar.dma_start(out=wout_raw[:], in_=Wout.rearrange("(t p) n -> p t n", p=P))
-        for step in range(RAW_BUFS):
-            load(step)
-        prepare(0, list)
-        load(RAW_BUFS)
+        nc.sync.dma_start(out=bout_padded[0:1, :], in_=bout.rearrange("(o n) -> o n", o=1))
+        load_weights(0)
+        load_hidden(1)
+        load_weights(1)
+        nc.sync.dma_start(out=wout_raw[:], in_=Wout.rearrange("(t p) n -> p t n", p=P))
+        start_loads(-1)
 
         bias_rows_f32 = consts.tile([P, P], F32)
-        nc.vector.tensor_copy(out=bias_rows_f32[:], in_=bias_rows[:])
+        nc.gpsimd.tensor_copy(out=bias_rows_f32[:], in_=bias_rows[:])
         bias_t = banks.tile([P, P], F32, tag="sum1_0")
         nc.tensor.transpose(bias_t[:], bias_rows_f32[:], identity[:])
         bias_cols = consts.tile([P, PACK], F32)
@@ -196,15 +209,20 @@ def tile_distancefusionblock_pb_k_kernel(tc, gv, ga, Wmv, bmv, Wma, bma, Wout, b
         bout_rows = consts.tile([P, FEATURES], F32)
         nc.vector.tensor_copy(out=bout_rows[:], in_=bout_psum[:])
 
+        prepare(0, list)
+        start_loads(0)
+
         wout_grouped = consts.tile([P, FEATURES, PACK], BF16, align_bytes=64)
-        nc.vector.tensor_copy(out=wout_grouped[:], in_=wout_raw[:].rearrange("p t n -> p n t"))
         wout_codes = consts.tile([P, FEATURES], U32, align_bytes=64)
         wout_scales = consts.tile([P, FEATURES], U8, align_bytes=64)
-        nc.vector.quantize_mx(
-            out=wout_codes[:].bitcast(FP8X4),
-            scales=wout_scales[:],
-            in_=wout_grouped[:].rearrange("p n t -> p (n t)"),
-        )
+
+        def quantise_wout():
+            nc.vector.tensor_copy(out=wout_grouped[:], in_=wout_raw[:].rearrange("p t n -> p n t"))
+            nc.vector.quantize_mx(
+                out=wout_codes[:].bitcast(FP8X4),
+                scales=wout_scales[:],
+                in_=wout_grouped[:].rearrange("p n t -> p (n t)"),
+            )
 
         joined = consts.tile([P, PACK, TOKENS], BF16)
 
@@ -224,21 +242,21 @@ def tile_distancefusionblock_pb_k_kernel(tc, gv, ga, Wmv, bmv, Wma, bma, Wout, b
         waiting = []
 
         def some_passes():
-            for step, j in waiting[:PE_RUN]:
-                multiply(step, j)
+            for block, j in waiting[:PE_RUN]:
+                multiply(block, j)
             waiting[:] = waiting[PE_RUN:]
 
-        for step in range(len(STEPS)):
-            if step + 1 < len(STEPS):
-                prepare(step + 1, some_passes)
-            if step + 1 + RAW_BUFS < len(STEPS):
-                load(step + 1 + RAW_BUFS)
-            if step >= 2 and STEPS[step - 2][:2] == (0, BLOCKS_PER_STREAM - 1):
+        for block in range(len(BLOCKS)):
+            if block + 1 < len(BLOCKS):
+                prepare(block + 1, some_passes)
+            start_loads(block + 1)
+            if block == 0:
+                quantise_wout()
+            if block >= 2 and BLOCKS[block - 1][0] > BLOCKS[block - 2][0]:
                 leave(0)
-            waiting += [(step, j) for j in range(STEPS[step][3])]
-            if step + 2 >= len(STEPS) or STEPS[step + 2][2] > 0:
-                while waiting:
-                    some_passes()
+            waiting += [(block, j) for j in range(BLOCKS[block][2])]
+        while waiting:
+            some_passes()
         leave(1)
 
         joined_grouped = consts.tile([P, TOKENS, PACK], BF16, align_bytes=64)

@@ -24,12 +24,12 @@ FEATURE_TILES = FEATURES // P
 STREAMS = 2
 PASSES_PER_STREAM = HIDDEN // K_PASS
 BLOCK_PASSES = ((2, 2) + 7 * (4,), 7 * (4,) + (2, 1, 1))
-HIDDEN_LOADS = ((2, 2, 4, 8, 8, 8), (8, 8, 8, 4, 2, 1, 1))
+HIDDEN_LOADS = BLOCK_PASSES
 QUANT_PASSES = 2
 PE_RUN = 2
 RUN = 4
 WEIGHT_BUFS = 6
-HIDDEN_BUFS = 4
+HIDDEN_BUFS = 6
 VECTOR_COLUMNS = FEATURES * 5 // 8
 
 
@@ -194,7 +194,9 @@ def tile_distancefusionblock_pb_k_kernel(tc, gv, ga, Wmv, bmv, Wma, bma, Wout, b
         load_weights(0)
         load_hidden(1)
         load_weights(1)
-        nc.sync.dma_start(out=wout_raw[:], in_=Wout.rearrange("(t p) n -> p t n", p=P))
+        wout_rows = Wout.rearrange("(s f p) n -> f p s n", s=STREAMS, p=P)
+        for f in range(FEATURE_TILES):
+            nc.sync.dma_start(out=wout_raw[:, f * STREAMS : (f + 1) * STREAMS, :], in_=wout_rows[f])
         start_loads(-1)
 
         bias_rows_f32 = consts.tile([P, P], F32)
@@ -224,20 +226,25 @@ def tile_distancefusionblock_pb_k_kernel(tc, gv, ga, Wmv, bmv, Wma, bma, Wout, b
                 in_=wout_grouped[:].rearrange("p n t -> p (n t)"),
             )
 
-        joined = consts.tile([P, PACK, TOKENS], BF16)
+        joined = consts.tile([P, TOKENS, PACK], BF16, align_bytes=64)
 
         def leave(stream):
-            t = stream * FEATURE_TILES
-            nc.scalar.activation(
-                out=joined[:, t, :], in_=sums[stream, 0][:], func=IDENTITY, bias=bias_cols[:, t : t + 1]
-            )
-            nc.vector.tensor_scalar(
-                out=joined[:, t + 1, :],
-                in0=sums[stream, 1][:],
-                scalar1=bias_cols[:, t + 1 : t + 2],
-                scalar2=None,
-                op0=ADD,
-            )
+            c = stream * FEATURE_TILES
+            for b in range(BATCH):
+                tokens = slice(b * P, (b + 1) * P)
+                nc.scalar.activation(
+                    out=joined[:, tokens, stream],
+                    in_=sums[stream, 0][:, tokens],
+                    func=IDENTITY,
+                    bias=bias_cols[:, c : c + 1],
+                )
+                nc.vector.tensor_scalar(
+                    out=joined[:, tokens, STREAMS + stream],
+                    in0=sums[stream, 1][:, tokens],
+                    scalar1=bias_cols[:, c + 1 : c + 2],
+                    scalar2=None,
+                    op0=ADD,
+                )
 
         waiting = []
 
@@ -259,15 +266,15 @@ def tile_distancefusionblock_pb_k_kernel(tc, gv, ga, Wmv, bmv, Wma, bma, Wout, b
             some_passes()
         leave(1)
 
-        joined_grouped = consts.tile([P, TOKENS, PACK], BF16, align_bytes=64)
-        nc.vector.tensor_copy(out=joined_grouped[:], in_=joined[:].rearrange("p t w -> p w t"))
         joined_codes = consts.tile([P, TOKENS], U32, align_bytes=64)
         joined_scales = consts.tile([P, TOKENS], U8, align_bytes=64)
-        nc.vector.quantize_mx(
-            out=joined_codes[:].bitcast(FP8X4),
-            scales=joined_scales[:],
-            in_=joined_grouped[:].rearrange("p w t -> p (w t)"),
-        )
+        for b in range(BATCH):
+            tokens = slice(b * P, (b + 1) * P)
+            nc.vector.quantize_mx(
+                out=joined_codes[:, tokens].bitcast(FP8X4),
+                scales=joined_scales[:, tokens],
+                in_=joined[:, tokens, :].rearrange("p w t -> p (w t)"),
+            )
         for b in range(BATCH):
             rows = slice(b * P, (b + 1) * P)
             fused = banks.tile([P, FEATURES], F32, tag="sum0_%d" % b)

@@ -23,45 +23,51 @@ FEATURES = 256
 FEATURE_TILES = FEATURES // P
 STREAMS = 2
 PASSES_PER_STREAM = HIDDEN // K_PASS
-BLOCK_PASSES = ((2, 2) + 7 * (4,), 7 * (4,) + (2, 1, 1))
-HIDDEN_LOADS = BLOCK_PASSES
 QUANT_PASSES = 2
-PE_RUN = 2
 RUN = 4
-WEIGHT_BUFS = 6
-HIDDEN_BUFS = 6
+BANK_HALVES = 4
+LAST_ITEMS = 4
+MULTIPLY_RUN = 4
+WEIGHT_BUFS = 5
+HIDDEN_BUFS = 5
+WEIGHT_CODES_BUFS = 6
 VECTOR_COLUMNS = FEATURES * 5 // 8
 
 
-def list_pieces(passes_of):
-    pieces = []
+def list_items():
+    both = tuple(range(BATCH))
+    small_first = (2, 2, 4)
+    small_last = (4, 2, 1, 1)
+    items = []
     for stream in range(STREAMS):
         first = 0
-        for passes in passes_of[stream]:
-            pieces.append((stream, first, passes))
+        for passes in small_first if stream == 0 else ():
+            items += [("hidden", stream, first, passes, both), ("weights", stream, first, passes)]
             first += passes
-        assert first == PASSES_PER_STREAM
-    return pieces
+        last = PASSES_PER_STREAM - (sum(small_last) if stream == STREAMS - 1 else 0)
+        for pair in range(first, last, 8):
+            for b in both:
+                items += [("hidden", stream, pair, 8, (b,)), ("weights", stream, pair + 4 * b, 4)]
+        first = last
+        for passes in small_last if stream == STREAMS - 1 else ():
+            items += [("hidden", stream, first, passes, both), ("weights", stream, first, passes)]
+            first += passes
+    return items
 
 
-BLOCKS = list_pieces(BLOCK_PASSES)
-HIDDEN_PIECES = list_pieces(HIDDEN_LOADS)
-
-
-def blocks_of(piece):
-    stream, first, passes = piece
-    return [i for i, (s, f, p) in enumerate(BLOCKS) if s == stream and first <= f < first + passes]
+ITEMS = list_items()
 
 
 def list_loads():
     loads = []
-    for piece_index, piece in enumerate(HIDDEN_PIECES):
-        blocks = blocks_of(piece)
-        reused = piece_index - HIDDEN_BUFS
-        loads.append(("hidden", piece_index, blocks_of(HIDDEN_PIECES[reused])[-1] if reused >= 0 else -1))
-        for block in blocks:
-            loads.append(("weights", block, block - WEIGHT_BUFS))
+    places = {"hidden": [], "weights": []}
+    bufs = {"hidden": HIDDEN_BUFS, "weights": WEIGHT_BUFS}
+    for i, item in enumerate(ITEMS):
+        before = places[item[0]]
+        loads.append((i, before[-bufs[item[0]]] if len(before) >= bufs[item[0]] else -1))
+        before += [i]
     return loads
+
 
 FLOPS = 2 * TOKENS * FEATURES * (STREAMS * HIDDEN + STREAMS * FEATURES)
 
@@ -82,28 +88,34 @@ def tile_distancefusionblock_pb_k_kernel(tc, gv, ga, Wmv, bmv, Wma, bma, Wout, b
         ctx.enter_context(tc.manual_schedule())
 
         raw_tiles = {}
+        hidden_tiles = {}
         operands = {}
         sums = {}
 
-        def load_hidden(index):
-            stream, first, passes = HIDDEN_PIECES[index]
+        def load(i):
+            kind, stream, first, passes = ITEMS[i][:4]
             k_rows = slice(first * K_PASS, (first + passes) * K_PASS)
-            g_raw = raw.tile([P, BATCH, passes * K_PASS], BF16, bufs=HIDDEN_BUFS)
-            nc.sync.dma_start(out=g_raw[:], in_=hidden[stream][:, :, k_rows].rearrange("b r k -> r b k"))
-            for block in blocks_of(HIDDEN_PIECES[index]):
-                raw_tiles["g", block] = (g_raw, BLOCKS[block][1] - first)
+            if kind == "hidden":
+                entries = ITEMS[i][4]
+                g_raw = raw.tile([P, len(entries), passes * K_PASS], BF16, bufs=HIDDEN_BUFS)
+                nc.sync.dma_start(
+                    out=g_raw[:],
+                    in_=hidden[stream][entries[0] : entries[-1] + 1, :, k_rows].rearrange("b r k -> r b k"),
+                )
+                raw_tiles[i] = g_raw
+            else:
+                w_raw = raw.tile([P, passes, PACK, FEATURES], BF16, bufs=WEIGHT_BUFS)
+                nc.sync.dma_start(
+                    out=w_raw[:].rearrange("p j t n -> p j (t n)"),
+                    in_=weights[stream][k_rows, :].rearrange("(j p t) n -> p j (t n)", j=passes, p=P, t=PACK),
+                )
+                raw_tiles[i] = w_raw
 
-        def load_weights(block):
-            stream, first, passes = BLOCKS[block]
-            k_rows = slice(first * K_PASS, (first + passes) * K_PASS)
-            w_raw = raw.tile([P, passes, PACK, FEATURES], BF16, bufs=WEIGHT_BUFS)
-            nc.sync.dma_start(
-                out=w_raw[:].rearrange("p j t n -> p j (t n)"),
-                in_=weights[stream][k_rows, :].rearrange("(j p t) n -> p j (t n)", j=passes, p=P, t=PACK),
-            )
-            raw_tiles["w", block] = w_raw
-
-        def quantise(values, codes, scales, passes):
+        def quantise(kind, stream, first, passes, values):
+            width = TOKENS if kind == "hidden" else FEATURES
+            bufs = 3 if kind == "hidden" else WEIGHT_CODES_BUFS
+            codes = quantised.tile([P, passes, width], U32, align_bytes=64, tag=kind + "_codes", bufs=bufs)
+            scales = quantised.tile([P, passes, width], U8, align_bytes=64, tag=kind + "_scales", bufs=bufs)
             for j in range(0, passes, QUANT_PASSES):
                 some = slice(j, min(j + QUANT_PASSES, passes))
                 nc.vector.quantize_mx(
@@ -111,57 +123,62 @@ def tile_distancefusionblock_pb_k_kernel(tc, gv, ga, Wmv, bmv, Wma, bma, Wout, b
                     scales=scales[:, some, :].rearrange("p j w -> p (j w)"),
                     in_=values[:, some, :].rearrange("p j v -> p (j v)"),
                 )
-
-        def prepare(block, between):
-            stream, first, passes = BLOCKS[block]
-            g_raw, g_first = raw_tiles["g", block]
-            w_raw = raw_tiles["w", block]
-
-            g_grouped = grouped.tile([P, passes, TOKENS * PACK], BF16, align_bytes=64)
             for j in range(passes):
-                words = transposed.tile([P, BATCH, HALVES, P], F32)
-                for b in range(BATCH):
-                    g_words = g_raw[:, b, :].bitcast(F32).rearrange("r (j p u) -> r j u p", p=P, u=HALVES)
-                    for u in range(HALVES):
-                        nc.tensor.transpose(words[:, b, u, :], g_words[:, g_first + j, u, :], identity[:])
-                nc.scalar.copy(
-                    out=g_grouped[:, j, :].bitcast(F32).rearrange("p (b r u) -> p b r u", b=BATCH, u=HALVES),
-                    in_=words[:].rearrange("p b u r -> p b r u"),
-                )
-                if (j + 1) % PE_RUN == 0 or j == passes - 1:
-                    between()
+                operands[kind, stream, first + j] = (codes, scales, j)
 
-            w_grouped = grouped.tile([P, passes, FEATURES * PACK], BF16, align_bytes=64)
+        def take_hidden(i):
+            stream, first, passes, entries = ITEMS[i][1:]
+            g_raw = raw_tiles[i]
+            if entries[0] == 0:
+                hidden_tiles[stream, first] = grouped.tile(
+                    [P, passes, TOKENS * PACK], BF16, align_bytes=64, name="g_grouped", bufs=3
+                )
+            g_grouped = hidden_tiles[stream, first]
+            run = BANK_HALVES // (HALVES * len(entries))
+            for j in range(0, passes, run):
+                words = transposed.tile([P, run, len(entries), HALVES, P], F32)
+                for r in range(run):
+                    for b in range(len(entries)):
+                        g_words = g_raw[:, b, :].bitcast(F32).rearrange("r (j p u) -> r j u p", p=P, u=HALVES)
+                        for u in range(HALVES):
+                            nc.tensor.transpose(words[:, r, b, u, :], g_words[:, j + r, u, :], identity[:])
+                out_words = g_grouped[:].bitcast(F32).rearrange("p j (b r u) -> p j b r u", b=BATCH, u=HALVES)
+                in_words = words[:].rearrange("p j b u r -> p j b r u")
+                if len(entries) == 1:
+                    nc.scalar.copy(out=out_words[:, j : j + run, entries[0]], in_=in_words[:, :, 0])
+                else:
+                    nc.scalar.copy(out=out_words[:, j], in_=in_words[:, 0])
+
+        def take_weights(i):
+            stream, first, passes = ITEMS[i][1:]
+            w_raw = raw_tiles[i]
+            w_grouped = grouped.tile([P, passes, FEATURES * PACK], BF16, align_bytes=64, bufs=3)
             dst = w_grouped[:].rearrange("p j (c i t) -> p j c t i", i=RUN, t=PACK)
             src = w_raw[:].rearrange("p j t (c i) -> p j c t i", i=RUN)
             cut = VECTOR_COLUMNS // RUN
             nc.vector.tensor_copy(out=dst[:, :, :cut], in_=src[:, :, :cut])
             nc.scalar.copy(out=dst[:, :, cut:], in_=src[:, :, cut:])
+            kind, stream_before, first_before, passes_before, entries = ITEMS[i - 1]
+            if entries[-1] == BATCH - 1:
+                quantise(kind, stream, first_before, passes_before, hidden_tiles[stream, first_before])
+            quantise("weights", stream, first, passes, w_grouped)
 
-            g_codes = quantised.tile([P, passes, TOKENS], U32, align_bytes=64)
-            g_scales = quantised.tile([P, passes, TOKENS], U8, align_bytes=64)
-            quantise(g_grouped, g_codes, g_scales, passes)
-            w_codes = quantised.tile([P, passes, FEATURES], U32, align_bytes=64)
-            w_scales = quantised.tile([P, passes, FEATURES], U8, align_bytes=64)
-            quantise(w_grouped, w_codes, w_scales, passes)
-            operands[block] = (g_codes, g_scales, w_codes, w_scales)
-
-        def multiply(block, j):
-            stream, first, passes = BLOCKS[block]
-            g_codes, g_scales, w_codes, w_scales = operands[block]
-            if first + j == 0:
+        def multiply(stream, j):
+            g_codes, g_scales, g = operands["hidden", stream, j]
+            w_codes, w_scales, w = operands["weights", stream, j]
+            if j == 0:
                 for f in range(FEATURE_TILES):
                     sums[stream, f] = banks.tile([P, TOKENS], F32, name="sum", tag="sum%d_%d" % (stream, f))
             for f in range(FEATURE_TILES):
                 columns = slice(f * P, (f + 1) * P)
                 nc.tensor.matmul_mx(
                     out=sums[stream, f][:],
-                    lhsT=w_codes[:, j, columns].bitcast(FP8X4),
-                    lhsT_scale=w_scales[:, j, columns],
-                    rhs=g_codes[:, j, :].bitcast(FP8X4),
-                    rhs_scale=g_scales[:, j, :],
-                    start=(first + j == 0),
-                    stop=(first + j == PASSES_PER_STREAM - 1),
+                    lhsT=w_codes[:, w, columns].bitcast(FP8X4),
+                    lhsT_scale=w_scales[:, w, columns],
+                    rhs=g_codes[:, g, :].bitcast(FP8X4),
+                    rhs_scale=g_scales[:, g, :],
+                    start=(j == 0),
+                    stop=(j == PASSES_PER_STREAM - 1),
                 )
 
         identity = consts.tile([P, P], F32)
@@ -176,24 +193,20 @@ def tile_distancefusionblock_pb_k_kernel(tc, gv, ga, Wmv, bmv, Wma, bma, Wout, b
         wout_raw = consts.tile([P, PACK, FEATURES], BF16)
         loads = list_loads()[4:]
 
-        def start_loads(prepared):
-            while loads and loads[0][2] <= prepared:
-                kind, index = loads[0][:2]
+        def start_loads(taken):
+            while loads and loads[0][1] <= taken:
+                load(loads[0][0])
                 loads[:] = loads[1:]
-                if kind == "hidden":
-                    load_hidden(index)
-                else:
-                    load_weights(index)
 
-        load_hidden(0)
+        load(0)
         nc.sync.dma_start(out=bias_rows[0:FEATURE_TILES, :], in_=bmv.rearrange("(f p) -> f p", p=P))
         nc.sync.dma_start(
             out=bias_rows[FEATURE_TILES : 2 * FEATURE_TILES, :], in_=bma.rearrange("(f p) -> f p", p=P)
         )
         nc.sync.dma_start(out=bout_padded[0:1, :], in_=bout.rearrange("(o n) -> o n", o=1))
-        load_weights(0)
-        load_hidden(1)
-        load_weights(1)
+        load(1)
+        load(2)
+        load(3)
         wout_rows = Wout.rearrange("(s f p) n -> f p s n", s=STREAMS, p=P)
         for f in range(FEATURE_TILES):
             nc.sync.dma_start(out=wout_raw[:, f * STREAMS : (f + 1) * STREAMS, :], in_=wout_rows[f])
@@ -210,9 +223,6 @@ def tile_distancefusionblock_pb_k_kernel(tc, gv, ga, Wmv, bmv, Wma, bma, Wout, b
         nc.tensor.matmul(bout_psum[:], lhsT=ones[:], rhs=bout_padded[:], start=True, stop=True)
         bout_rows = consts.tile([P, FEATURES], F32)
         nc.vector.tensor_copy(out=bout_rows[:], in_=bout_psum[:])
-
-        prepare(0, list)
-        start_loads(0)
 
         wout_grouped = consts.tile([P, FEATURES, PACK], BF16, align_bytes=64)
         wout_codes = consts.tile([P, FEATURES], U32, align_bytes=64)
@@ -247,24 +257,39 @@ def tile_distancefusionblock_pb_k_kernel(tc, gv, ga, Wmv, bmv, Wma, bma, Wout, b
                 )
 
         waiting = []
+        summed = []
 
-        def some_passes():
-            for block, j in waiting[:PE_RUN]:
-                multiply(block, j)
-            waiting[:] = waiting[PE_RUN:]
+        def multiply_some(count):
+            for stream, j in waiting[:count]:
+                multiply(stream, j)
+                if j == PASSES_PER_STREAM - 1:
+                    summed.append(stream)
+            waiting[:] = waiting[count:]
 
-        for block in range(len(BLOCKS)):
-            if block + 1 < len(BLOCKS):
-                prepare(block + 1, some_passes)
-            start_loads(block + 1)
-            if block == 0:
+        def leave_summed():
+            for stream in summed:
+                leave(stream)
+            summed[:] = []
+
+        queued = []
+        for i, item in enumerate(ITEMS):
+            if item[0] == "hidden":
+                take_hidden(i)
+                if i < len(ITEMS) - LAST_ITEMS:
+                    multiply_some(MULTIPLY_RUN)
+            else:
+                take_weights(i)
+                leave_summed()
+                if ITEMS[i - 1][4][-1] == BATCH - 1:
+                    stream, first, passes = item[1:]
+                    news = [(stream, j) for j in range(first + passes) if (stream, j) not in queued]
+                    waiting += news
+                    queued += news
+            start_loads(i)
+            if i == 3:
                 quantise_wout()
-            if block >= 2 and BLOCKS[block - 1][0] > BLOCKS[block - 2][0]:
-                leave(0)
-            waiting += [(block, j) for j in range(BLOCKS[block][2])]
-        while waiting:
-            some_passes()
-        leave(1)
+        multiply_some(len(waiting))
+        leave_summed()
 
         joined_codes = consts.tile([P, TOKENS], U32, align_bytes=64)
         joined_scales = consts.tile([P, TOKENS], U8, align_bytes=64)

@@ -24,7 +24,7 @@ FEATURE_TILES = FEATURES // P
 STREAMS = 2
 PASSES_PER_STREAM = HIDDEN // K_PASS
 QUANT_PASSES = 2
-RUN = 4
+RUN = 8
 BANK_HALVES = 4
 LAST_ITEMS = 4
 MULTIPLY_RUN = 4

from contextlib import ExitStack

import concourse.masks as masks
import concourse.mybir as mybir

BF16 = mybir.dt.bfloat16
F32 = mybir.dt.float32
U32 = mybir.dt.uint32
U8 = mybir.dt.uint8
FP8X4 = mybir.dt.float8_e4m3fn_x4
ADD = mybir.AluOpType.add
IDENTITY = mybir.ActivationFunctionType.Identity

P = 128
PACK = 4
PAIR = 2
HALVES = PACK // PAIR
K_PASS = P * PACK
BATCH = 2
TOKENS = BATCH * P
HIDDEN = 16384
FEATURES = 256
FEATURE_TILES = FEATURES // P
STREAMS = 2
PASSES_PER_STREAM = HIDDEN // K_PASS
QUANT_PASSES = 2
RUN = 8
BANK_HALVES = 4
LAST_ITEMS = 4
MULTIPLY_RUN = 4
WEIGHT_BUFS = 5
HIDDEN_BUFS = 5
WEIGHT_CODES_BUFS = 6
VECTOR_COLUMNS = FEATURES * 5 // 8


def list_items():
    both = tuple(range(BATCH))
    small_first = (2, 2, 4)
    small_last = (4, 2, 1, 1)
    items = []
    for stream in range(STREAMS):
        first = 0
        for passes in small_first if stream == 0 else ():
            items += [("hidden", stream, first, passes, both), ("weights", stream, first, passes)]
            first += passes
        last = PASSES_PER_STREAM - (sum(small_last) if stream == STREAMS - 1 else 0)
        for pair in range(first, last, 8):
            for b in both:
                items += [("hidden", stream, pair, 8, (b,)), ("weights", stream, pair + 4 * b, 4)]
        first = last
        for passes in small_last if stream == STREAMS - 1 else ():
            items += [("hidden", stream, first, passes, both), ("weights", stream, first, passes)]
            first += passes
    return items


ITEMS = list_items()


def list_loads():
    loads = []
    places = {"hidden": [], "weights": []}
    bufs = {"hidden": HIDDEN_BUFS, "weights": WEIGHT_BUFS}
    for i, item in enumerate(ITEMS):
        before = places[item[0]]
        loads.append((i, before[-bufs[item[0]]] if len(before) >= bufs[item[0]] else -1))
        before += [i]
    return loads


FLOPS = 2 * TOKENS * FEATURES * (STREAMS * HIDDEN + STREAMS * FEATURES)


def tile_distancefusionblock_pb_k_kernel(tc, gv, ga, Wmv, bmv, Wma, bma, Wout, bout, out):
    nc = tc.nc
    hidden = (gv, ga)
    weights = (Wmv, Wma)

    with ExitStack() as ctx:
        consts = ctx.enter_context(tc.tile_pool(name="consts", bufs=1))
        raw = ctx.enter_context(tc.tile_pool(name="raw", bufs=1))
        grouped = ctx.enter_context(tc.tile_pool(name="grouped", bufs=3))
        quantised = ctx.enter_context(tc.tile_pool(name="quantised", bufs=4))
        results = ctx.enter_context(tc.tile_pool(name="results", bufs=BATCH))
        transposed = ctx.enter_context(tc.psum_pool(name="transposed", bufs=4))
        banks = ctx.enter_context(tc.psum_pool(name="banks", bufs=1))
        ctx.enter_context(tc.manual_schedule())

        raw_tiles = {}
        hidden_tiles = {}
        operands = {}
        sums = {}

        def load(i):
            kind, stream, first, passes = ITEMS[i][:4]
            k_rows = slice(first * K_PASS, (first + passes) * K_PASS)
            if kind == "hidden":
                entries = ITEMS[i][4]
                g_raw = raw.tile([P, len(entries), passes * K_PASS], BF16, bufs=HIDDEN_BUFS)
                nc.sync.dma_start(
                    out=g_raw[:],
                    in_=hidden[stream][entries[0] : entries[-1] + 1, :, k_rows].rearrange("b r k -> r b k"),
                )
                raw_tiles[i] = g_raw
            else:
                w_raw = raw.tile([P, passes, PACK, FEATURES], BF16, bufs=WEIGHT_BUFS)
                nc.sync.dma_start(
                    out=w_raw[:].rearrange("p j t n -> p j (t n)"),
                    in_=weights[stream][k_rows, :].rearrange("(j p t) n -> p j (t n)", j=passes, p=P, t=PACK),
                )
                raw_tiles[i] = w_raw

        def quantise(kind, stream, first, passes, values):
            width = TOKENS if kind == "hidden" else FEATURES
            bufs = 3 if kind == "hidden" else WEIGHT_CODES_BUFS
            codes = quantised.tile([P, passes, width], U32, align_bytes=64, tag=kind + "_codes", bufs=bufs)
            scales = quantised.tile([P, passes, width], U8, align_bytes=64, tag=kind + "_scales", bufs=bufs)
            for j in range(0, passes, QUANT_PASSES):
                some = slice(j, min(j + QUANT_PASSES, passes))
                nc.vector.quantize_mx(
                    out=codes[:, some, :].rearrange("p j w -> p (j w)").bitcast(FP8X4),
                    scales=scales[:, some, :].rearrange("p j w -> p (j w)"),
                    in_=values[:, some, :].rearrange("p j v -> p (j v)"),
                )
            for j in range(passes):
                operands[kind, stream, first + j] = (codes, scales, j)

        def take_hidden(i):
            stream, first, passes, entries = ITEMS[i][1:]
            g_raw = raw_tiles[i]
            if entries[0] == 0:
                hidden_tiles[stream, first] = grouped.tile(
                    [P, passes, TOKENS * PACK], BF16, align_bytes=64, name="g_grouped", bufs=3
                )
            g_grouped = hidden_tiles[stream, first]
            run = BANK_HALVES // (HALVES * len(entries))
            for j in range(0, passes, run):
                words = transposed.tile([P, run, len(entries), HALVES, P], F32)
                for r in range(run):
                    for b in range(len(entries)):
                        g_words = g_raw[:, b, :].bitcast(F32).rearrange("r (j p u) -> r j u p", p=P, u=HALVES)
                        for u in range(HALVES):
                            nc.tensor.transpose(words[:, r, b, u, :], g_words[:, j + r, u, :], identity[:])
                out_words = g_grouped[:].bitcast(F32).rearrange("p j (b r u) -> p j b r u", b=BATCH, u=HALVES)
                in_words = words[:].rearrange("p j b u r -> p j b r u")
                if len(entries) == 1:
                    nc.scalar.copy(out=out_words[:, j : j + run, entries[0]], in_=in_words[:, :, 0])
                else:
                    nc.scalar.copy(out=out_words[:, j], in_=in_words[:, 0])

        def take_weights(i):
            stream, first, passes = ITEMS[i][1:]
            w_raw = raw_tiles[i]
            w_grouped = grouped.tile([P, passes, FEATURES * PACK], BF16, align_bytes=64, bufs=3)
            dst = w_grouped[:].rearrange("p j (c i t) -> p j c t i", i=RUN, t=PACK)
            src = w_raw[:].rearrange("p j t (c i) -> p j c t i", i=RUN)
            cut = VECTOR_COLUMNS // RUN
            nc.vector.tensor_copy(out=dst[:, :, :cut], in_=src[:, :, :cut])
            nc.scalar.copy(out=dst[:, :, cut:], in_=src[:, :, cut:])
            kind, stream_before, first_before, passes_before, entries = ITEMS[i - 1]
            if entries[-1] == BATCH - 1:
                quantise(kind, stream, first_before, passes_before, hidden_tiles[stream, first_before])
            quantise("weights", stream, first, passes, w_grouped)

        def multiply(stream, j):
            g_codes, g_scales, g = operands["hidden", stream, j]
            w_codes, w_scales, w = operands["weights", stream, j]
            if j == 0:
                for f in range(FEATURE_TILES):
                    sums[stream, f] = banks.tile([P, TOKENS], F32, name="sum", tag="sum%d_%d" % (stream, f))
            for f in range(FEATURE_TILES):
                columns = slice(f * P, (f + 1) * P)
                nc.tensor.matmul_mx(
                    out=sums[stream, f][:],
                    lhsT=w_codes[:, w, columns].bitcast(FP8X4),
                    lhsT_scale=w_scales[:, w, columns],
                    rhs=g_codes[:, g, :].bitcast(FP8X4),
                    rhs_scale=g_scales[:, g, :],
                    start=(j == 0),
                    stop=(j == PASSES_PER_STREAM - 1),
                )

        identity = consts.tile([P, P], F32)
        masks.make_identity(nc, identity[:])

        bias_rows = consts.tile([P, P], BF16)
        nc.vector.memset(bias_rows[:], 0.0)
        bout_padded = consts.tile([P, FEATURES], BF16)
        nc.vector.memset(bout_padded[:], 0.0)
        ones = consts.tile([P, P], BF16)
        nc.vector.memset(ones[:], 1.0)
        wout_raw = consts.tile([P, PACK, FEATURES], BF16)
        loads = list_loads()[4:]

        def start_loads(taken):
            while loads and loads[0][1] <= taken:
                load(loads[0][0])
                loads[:] = loads[1:]

        load(0)
        nc.sync.dma_start(out=bias_rows[0:FEATURE_TILES, :], in_=bmv.rearrange("(f p) -> f p", p=P))
        nc.sync.dma_start(
            out=bias_rows[FEATURE_TILES : 2 * FEATURE_TILES, :], in_=bma.rearrange("(f p) -> f p", p=P)
        )
        nc.sync.dma_start(out=bout_padded[0:1, :], in_=bout.rearrange("(o n) -> o n", o=1))
        load(1)
        load(2)
        load(3)
        wout_rows = Wout.rearrange("(s f p) n -> f p s n", s=STREAMS, p=P)
        for f in range(FEATURE_TILES):
            nc.sync.dma_start(out=wout_raw[:, f * STREAMS : (f + 1) * STREAMS, :], in_=wout_rows[f])
        start_loads(-1)

        bias_rows_f32 = consts.tile([P, P], F32)
        nc.gpsimd.tensor_copy(out=bias_rows_f32[:], in_=bias_rows[:])
        bias_t = banks.tile([P, P], F32, tag="sum1_0")
        nc.tensor.transpose(bias_t[:], bias_rows_f32[:], identity[:])
        bias_cols = consts.tile([P, PACK], F32)
        nc.vector.tensor_copy(out=bias_cols[:], in_=bias_t[:, 0:PACK])

        bout_psum = banks.tile([P, FEATURES], F32, tag="sum1_1")
        nc.tensor.matmul(bout_psum[:], lhsT=ones[:], rhs=bout_padded[:], start=True, stop=True)
        bout_rows = consts.tile([P, FEATURES], F32)
        nc.vector.tensor_copy(out=bout_rows[:], in_=bout_psum[:])

        wout_grouped = consts.tile([P, FEATURES, PACK], BF16, align_bytes=64)
        wout_codes = consts.tile([P, FEATURES], U32, align_bytes=64)
        wout_scales = consts.tile([P, FEATURES], U8, align_bytes=64)

        def quantise_wout():
            nc.vector.tensor_copy(out=wout_grouped[:], in_=wout_raw[:].rearrange("p t n -> p n t"))
            nc.vector.quantize_mx(
                out=wout_codes[:].bitcast(FP8X4),
                scales=wout_scales[:],
                in_=wout_grouped[:].rearrange("p n t -> p (n t)"),
            )

        joined = consts.tile([P, TOKENS, PACK], BF16, align_bytes=64)

        def leave(stream):
            c = stream * FEATURE_TILES
            for b in range(BATCH):
                tokens = slice(b * P, (b + 1) * P)
                nc.scalar.activation(
                    out=joined[:, tokens, stream],
                    in_=sums[stream, 0][:, tokens],
                    func=IDENTITY,
                    bias=bias_cols[:, c : c + 1],
                )
                nc.vector.tensor_scalar(
                    out=joined[:, tokens, STREAMS + stream],
                    in0=sums[stream, 1][:, tokens],
                    scalar1=bias_cols[:, c + 1 : c + 2],
                    scalar2=None,
                    op0=ADD,
                )

        waiting = []
        summed = []

        def multiply_some(count):
            for stream, j in waiting[:count]:
                multiply(stream, j)
                if j == PASSES_PER_STREAM - 1:
                    summed.append(stream)
            waiting[:] = waiting[count:]

        def leave_summed():
            for stream in summed:
                leave(stream)
            summed[:] = []

        queued = []
        for i, item in enumerate(ITEMS):
            if item[0] == "hidden":
                take_hidden(i)
                if i < len(ITEMS) - LAST_ITEMS:
                    multiply_some(MULTIPLY_RUN)
            else:
                take_weights(i)
                leave_summed()
                if ITEMS[i - 1][4][-1] == BATCH - 1:
                    stream, first, passes = item[1:]
                    news = [(stream, j) for j in range(first + passes) if (stream, j) not in queued]
                    waiting += news
                    queued += news
            start_loads(i)
            if i == 3:
                quantise_wout()
        multiply_some(len(waiting))
        leave_summed()

        joined_codes = consts.tile([P, TOKENS], U32, align_bytes=64)
        joined_scales = consts.tile([P, TOKENS], U8, align_bytes=64)
        for b in range(BATCH):
            tokens = slice(b * P, (b + 1) * P)
            nc.vector.quantize_mx(
                out=joined_codes[:, tokens].bitcast(FP8X4),
                scales=joined_scales[:, tokens],
                in_=joined[:, tokens, :].rearrange("p w t -> p (w t)"),
            )
        for b in range(BATCH):
            rows = slice(b * P, (b + 1) * P)
            fused = banks.tile([P, FEATURES], F32, tag="sum0_%d" % b)
            nc.tensor.matmul_mx(
                out=fused[:],
                lhsT=joined_codes[:, rows].bitcast(FP8X4),
                lhsT_scale=joined_scales[:, rows],
                rhs=wout_codes[:].bitcast(FP8X4),
                rhs_scale=wout_scales[:],
                start=True,
                stop=True,
            )
            result = results.tile([P, FEATURES], F32)
            nc.vector.tensor_tensor(out=result[:], in0=fused[:], in1=bout_rows[:], op=ADD)
            nc.sync.dma_start(out=out[b], in_=result[:])
